import numpy as np
import ml_dtypes


def mxq(x, axis, fmt="e4m3"):
    dtype, down = {"e4m3": (ml_dtypes.float8_e4m3fn, 7), "e5m2": (ml_dtypes.float8_e5m2, 14)}[fmt]
    v = np.moveaxis(np.asarray(x, np.float32).astype(ml_dtypes.bfloat16).astype(np.float64), axis, -1)
    blocks = v.reshape(v.shape[:-1] + (-1, 32))
    amax = np.abs(blocks).max(-1, keepdims=True)
    byte = np.maximum(np.where(amax > 0, np.frexp(amax)[1] - 1 + 127, 0) - down, 1)
    scale = np.exp2(byte - 127.0)
    codes = (blocks / scale).astype(np.float32).astype(dtype).astype(np.float64)
    return np.moveaxis((codes * scale).reshape(v.shape), -1, axis)


WIDE = False


def mx_kscale(k):
    if not WIDE:
        return np.ones(k)
    levels = np.array([10, -10, 5, -5, 0])
    if k % 512:
        return np.exp2(np.random.permutation(np.resize(levels, k // 32))).repeat(32)
    a = np.empty((k // 512, 16))
    for p in range(k // 512):
        a[p, :8] = np.random.permutation(np.resize(levels, 8))
        for g in range(8):
            far = levels[np.abs(levels - a[p, g]) >= 10]
            a[p, g + 8] = far[np.random.randint(len(far))]
    return np.exp2(a.ravel()).repeat(32)


BF16 = ml_dtypes.bfloat16


def bf(x):
    return np.asarray(x, np.float32).astype(BF16)


def f64(x):
    return np.asarray(x).astype(np.float64)


B, IN, OUT, ND, R = 1024, 1024, 256, 8, 4
J = OUT * ND
GS = 16.0


def kernel_probs(x, c):
    x2 = np.sum(x * x, axis=-1, keepdims=True)
    c2 = np.sum(c * c, axis=-1)[None, :]
    d2 = x2 - 2.0 * (x @ c.T) + c2
    return np.exp(-d2 / 2.0)


def setup_inputs():
    s = mx_kscale(B)[:, None]
    uo = mx_kscale(J)[::ND]
    u = np.repeat(uo, ND)[:, None]
    p = np.random.standard_normal((R, IN)) / np.sqrt(IN)
    a = np.sqrt(2.0 / R)
    x0 = bf(np.random.standard_normal((B, R)) @ p * a)
    c0 = bf(np.random.standard_normal((J, R)) @ p * a)
    g = bf(np.random.standard_normal((B, OUT)) * np.exp2(np.random.randint(-6, 1, (B, 1))) * GS / s * uo[None, :])
    probs = kernel_probs(f64(x0), f64(c0))
    return {"x": bf(f64(x0) * s), "centers": bf(f64(c0) / u).reshape(OUT, ND, IN),
            "probs": np.asarray(probs, np.float32), "grad_out": g}


def reference(x, centers, probs, grad_out):
    x = f64(x)
    c = f64(centers).reshape(J, IN)
    pr = f64(probs).reshape(B, OUT, ND)
    hot = np.where(pr == np.max(pr, axis=-1, keepdims=True), 1.0, 0.0)
    hot = hot / np.sum(hot, axis=-1, keepdims=True)
    e = (f64(grad_out)[:, :, None] * (((ND + 1) * hot - 1.0) / ND) * pr).reshape(B, J)
    rb = np.sum(e, axis=1)
    rj = np.sum(e, axis=0)
    gx = (mxq(e, 1, "e5m2") @ mxq(c, 0, "e4m3")) - x * rb[:, None]
    gc = (mxq(e, 0, "e5m2").T @ mxq(x, 0, "e4m3")) - c * rj[:, None]
    return gx, gc.reshape(OUT, ND, IN)

@@ -1,0 +1,481 @@
+from contextlib import ExitStack
+
+import concourse.mybir as mybir
+from concourse.masks import make_identity
+
+B, IN, OUT, ND = 1024, 1024, 256, 8
+J = OUT * ND
+FLOPS = 2 * 2 * B * J * IN
+
+F32 = mybir.dt.float32
+BF16 = mybir.dt.bfloat16
+U32 = mybir.dt.uint32
+U8 = mybir.dt.uint8
+E4 = mybir.dt.float8_e4m3fn_x4
+E5 = mybir.dt.float8_e5m2_x4
+ALU = mybir.AluOpType
+ACT = mybir.ActivationFunctionType
+AX = mybir.AxisListType
+
+P = 128
+
+
+def tile_pnn_v_kernel(tc, x, centers, probs, grad_out, out_0, out_1):
+    nc = tc.nc
+    probs_v = probs.rearrange("(g p j) f -> p g j f", g=2, j=4)
+    grad_v = grad_out.rearrange("(g p j) o -> p g j o", g=2, j=4)
+    x_v = x.rearrange("(g p j) i -> p g j i", g=2, j=4)
+    c_v = centers.flatten_outer_dims().rearrange("(a q t) i -> q a t i", a=4, t=4)
+    out0_v = out_0.rearrange("(g p j) i -> p g j i", g=2, j=4)
+    out1_v = out_1.flatten_outer_dims().rearrange("(a q t) i -> q a t i", a=4, t=4)
+
+    order = [(0, 0), (1, 0), (0, 1), (1, 1), (0, 2), (0, 3), (1, 2), (1, 3)]
+    nblk = len(order)
+
+    with ExitStack() as ctx:
+        const = ctx.enter_context(tc.tile_pool(name="const", bufs=1))
+        keep = ctx.enter_context(tc.tile_pool(name="keep", bufs=1))
+        prp = ctx.enter_context(tc.tile_pool(name="prp", bufs=5))
+        work = ctx.enter_context(tc.tile_pool(name="work", bufs=2))
+        grp = ctx.enter_context(tc.tile_pool(name="grp", bufs=6))
+        stage = ctx.enter_context(tc.tile_pool(name="stage", bufs=3))
+        tp_ps = ctx.enter_context(tc.psum_pool(name="tp_ps", bufs=2))
+        acc_ps = ctx.enter_context(tc.psum_pool(name="acc_ps", bufs=5))
+        rj_ps = ctx.enter_context(tc.psum_pool(name="rj_ps", bufs=1))
+
+        ident = const.tile([P, P], F32, name="ident")
+        make_identity(nc, ident[:])
+        negones = const.tile([P, P], F32, name="negones")
+        nc.gpsimd.memset(negones[:], -1.0)
+        dummy = const.tile([P, 1], F32, name="dummy")
+        nc.scalar.activation(out=dummy[:], in_=negones[:, 0:1], func=ACT.Abs_reciprocal_sqrt)
+
+        gt = keep.tile([P, 2, 4, OUT], BF16, name="gt")
+        x_raw = []
+        xc = []
+        xs = []
+        for g in range(2):
+            xr = keep.tile([P, 4, IN], BF16, name="xraw%d" % g)
+            x_raw.append(xr)
+            xcg = keep.tile([P, IN], U32, name="xc%d" % g, align_bytes=64)
+            xc.append(xcg)
+            xsg = keep.tile([P, IN], U8, name="xs%d" % g, align_bytes=64)
+            xs.append(xsg)
+        c_raw = []
+        cc = []
+        cs = []
+        for a in range(4):
+            cr = keep.tile([P, 4, IN], BF16, name="craw%d" % a)
+            c_raw.append(cr)
+            cca = keep.tile([P, IN], U32, name="cc%d" % a, align_bytes=64)
+            cc.append(cca)
+            csa = keep.tile([P, IN], U8, name="cs%d" % a, align_bytes=64)
+            cs.append(csa)
+        e0c = {}
+        e0s = {}
+        e1c = {}
+        e1s = {}
+        for i in range(nblk):
+            t0 = keep.tile([P, 512], U32, name="e0c%d" % i, align_bytes=64)
+            e0c[order[i]] = t0
+            t1 = keep.tile([P, 512], U8, name="e0s%d" % i, align_bytes=64)
+            e0s[order[i]] = t1
+            t2 = keep.tile([P, 512], U32, name="e1c%d" % i, align_bytes=64)
+            e1c[order[i]] = t2
+            t3 = keep.tile([P, 512], U8, name="e1s%d" % i, align_bytes=64)
+            e1s[order[i]] = t3
+        rbp = keep.tile([P, 2, 4, 4], F32, name="rbp")
+        rbs = keep.tile([P, 2, 4], F32, name="rbs")
+        nrb = keep.tile([P, 2, 4], F32, name="nrb")
+        rjp = keep.tile([P, 2, 4, 4], F32, name="rjp")
+        nrj = keep.tile([P, 4, 4], F32, name="nrj")
+
+        pr_tiles = {}
+
+        def load_pr(i):
+            g, a = order[i]
+            pr = prp.tile([P, 4, 512], F32, name="pr", tag="pr")
+            nc.sync.dma_start(out=pr[:], in_=probs_v[:, g, :, 512 * a : 512 * a + 512])
+            pr_tiles[i] = pr
+
+        nc.sync.dma_start(out=gt[:], in_=grad_v)
+        load_pr(0)
+        load_pr(1)
+        nc.sync.dma_start(out=x_raw[0][:], in_=x_v[:, 0])
+        nc.sync.dma_start(out=x_raw[1][:], in_=x_v[:, 1])
+        load_pr(2)
+        for a in range(4):
+            nc.sync.dma_start(out=c_raw[a][:], in_=c_v[:, a])
+
+        prep = [(x_raw[g], xc[g], xs[g], h) for g in range(2) for h in range(2)]
+        prep.extend([(c_raw[a], cc[a], cs[a], h) for a in range(4) for h in range(2)])
+        prep_tiles = {}
+
+        def prep_copy(k):
+            raw, codes, scales, h = prep[k]
+            gq = grp.tile([P, 2048], BF16, name="gq", tag="grp", align_bytes=64)
+            nc.scalar.copy(
+                out=gq[:].rearrange("p (i t) -> p i t", t=4),
+                in_=raw[:, :, 512 * h : 512 * h + 512].rearrange("p t i -> p i t"),
+            )
+            prep_tiles[k] = gq
+
+        def prep_quant(k):
+            raw, codes, scales, h = prep[k]
+            nc.vector.quantize_mx(
+                out=codes[:, 512 * h : 512 * h + 512].bitcast(E4),
+                scales=scales[:, 512 * h : 512 * h + 512],
+                in_=prep_tiles[k][:],
+            )
+
+        st = {}
+
+        def a_max(i):
+            pr = pr_tiles[i]
+            m = work.tile([P, 4, 64], F32, name="m", tag="m")
+            nc.vector.tensor_reduce(
+                out=m[:], in_=pr[:].rearrange("p j (o d) -> p j o d", d=8), axis=AX.X, op=ALU.max
+            )
+            st[("m", i)] = m
+
+        def a_hot(i):
+            pr = pr_tiles[i]
+            hot = work.tile([P, 4, 8, 64], BF16, name="hot", tag="hot")
+            nc.vector.tensor_tensor(
+                out=hot[:],
+                in0=pr[:].rearrange("p j (o d) -> p j d o", d=8),
+                in1=st[("m", i)][:].unsqueeze(2).to_broadcast([P, 4, 8, 64]),
+                op=ALU.is_equal,
+            )
+            st[("hot", i)] = hot
+            kk = work.tile([P, 4, 8, 64], BF16, name="kk", tag="kk")
+            nc.scalar.mul(out=kk[:], in_=hot[:], mul=9.0)
+            st[("kk", i)] = kk
+
+        def a_s4(i):
+            hot = st[("hot", i)]
+            s4 = work.tile([P, 4, 4, 64], BF16, name="s4", tag="s4")
+            nc.vector.tensor_tensor(out=s4[:], in0=hot[:, :, 0:4, :], in1=hot[:, :, 4:8, :], op=ALU.add)
+            st[("s4", i)] = s4
+
+        def a_s2(i):
+            s4 = st[("s4", i)]
+            s2 = work.tile([P, 4, 2, 64], BF16, name="s2", tag="s2")
+            nc.vector.tensor_tensor(out=s2[:], in0=s4[:, :, 0:2, :], in1=s4[:, :, 2:4, :], op=ALU.add)
+            st[("s2", i)] = s2
+
+        def a_n(i):
+            s2 = st[("s2", i)]
+            n = work.tile([P, 4, 64], BF16, name="n", tag="n")
+            nc.vector.tensor_tensor(out=n[:], in0=s2[:, :, 0, :], in1=s2[:, :, 1, :], op=ALU.add)
+            st[("n", i)] = n
+
+        def a_n2(i):
+            n = st[("n", i)]
+            n2 = work.tile([P, 4, 64], BF16, name="n2", tag="n2")
+            nc.vector.tensor_tensor(out=n2[:], in0=n[:], in1=n[:], op=ALU.mult)
+            rt = work.tile([P, 4, 64], F32, name="rt", tag="rt")
+            nc.scalar.activation(out=rt[:], in_=n2[:], func=ACT.Abs_reciprocal_sqrt)
+            st[("rt", i)] = rt
+
+        def a_k(i):
+            kk = st[("kk", i)]
+            nc.vector.tensor_tensor(
+                out=kk[:], in0=kk[:], in1=st[("n", i)][:].unsqueeze(2).to_broadcast([P, 4, 8, 64]),
+                op=ALU.subtract,
+            )
+
+        def b_u(i):
+            u = work.tile([P, 4, 64], F32, name="u", tag="u")
+            nc.vector.scalar_tensor_tensor(
+                out=u[:], in0=st[("n", i)][:], scalar=1.0, in1=st[("rt", i)][:],
+                op0=ALU.subtract, op1=ALU.mult,
+            )
+            st[("u", i)] = u
+
+        def b_v(i):
+            g, a = order[i]
+            v = work.tile([P, 4, 64], F32, name="v", tag="v")
+            nc.vector.scalar_tensor_tensor(
+                out=v[:], in0=st[("u", i)][:], scalar=1.0, in1=gt[:, g, :, 64 * a : 64 * a + 64],
+                op0=ALU.subtract, op1=ALU.mult,
+            )
+            st[("v", i)] = v
+
+        def b_yr(eng, i, j_lo, j_hi):
+            prv = pr_tiles[i][:, j_lo:j_hi, :].rearrange("p j (o d) -> p j o d", d=8)
+            eng.tensor_tensor(
+                out=prv, in0=prv,
+                in1=st[("v", i)][:, j_lo:j_hi, :].unsqueeze(3).to_broadcast([P, j_hi - j_lo, 64, 8]),
+                op=ALU.mult,
+            )
+
+        def b_e(i, j):
+            g, a = order[i]
+            pr = pr_tiles[i]
+            if j == 0:
+                g0 = grp.tile([P, 2048], BF16, name="g0", tag="grp", align_bytes=64)
+                st[("g0", i)] = g0
+                rjw = rj_ps.tile([P, 512], F32, name="rjw", tag="rjw")
+                st[("rjw", i)] = rjw
+            g0v = st[("g0", i)][:].rearrange("q (j p t) -> q j p t", j=4, t=4)
+            ej = pr[:, j, :].rearrange("p (o d) -> p o d", d=8)
+            nc.vector.scalar_tensor_tensor(
+                out=ej, in0=st[("kk", i)][:, j, :, :].rearrange("p d o -> p o d"), scalar=-0.125, in1=ej,
+                op0=ALU.mult, op1=ALU.mult, accum_out=rbp[:, g, a, j : j + 1],
+            )
+            nc.tensor.matmul(
+                out=st[("rjw", i)][:], lhsT=negones[:], rhs=pr[:, j, :], start=(j == 0), stop=(j == 3)
+            )
+            tp = tp_ps.tile([P, 4, P], F32, name="tp", tag="tp")
+            for t in range(4):
+                nc.tensor.transpose(tp[:, t, :], pr[:, j, t:512:4], ident[:])
+            nc.scalar.copy(out=g0v[:, j], in_=tp[:].rearrange("q t p -> q p t"))
+
+        def b_rjs(i):
+            rjs = work.tile([P, 512], F32, name="rjs", tag="rjs")
+            nc.scalar.copy(out=rjs[:], in_=st[("rjw", i)][:])
+            st[("rjs", i)] = rjs
+
+        def b_rjt(i):
+            g, a = order[i]
+            rjs = st[("rjs", i)]
+            tpr = tp_ps.tile([P, 4, P], F32, name="tpr", tag="tp")
+            for t in range(4):
+                nc.tensor.transpose(tpr[:, t, :], rjs[:, t:512:4], ident[:])
+            nc.scalar.copy(out=rjp[:, g, a, :], in_=tpr[:, :, 0])
+
+        def b_g1(i, t_lo, t_hi):
+            if t_lo == 0:
+                g1 = grp.tile([P, 2048], BF16, name="g1", tag="grp", align_bytes=64)
+                st[("g1", i)] = g1
+            nc.scalar.copy(
+                out=st[("g1", i)][:, 512 * t_lo : 512 * t_hi].rearrange("p (t q j) -> p t q j", t=t_hi - t_lo, j=4),
+                in_=pr_tiles[i][:].rearrange("p j (q t) -> p t q j", t=4)[:, t_lo:t_hi],
+            )
+
+        def c_q0(i, j_lo, j_hi):
+            nc.vector.quantize_mx(
+                out=e0c[order[i]][:, 128 * j_lo : 128 * j_hi].bitcast(E5),
+                scales=e0s[order[i]][:, 128 * j_lo : 128 * j_hi],
+                in_=st[("g0", i)][:, 512 * j_lo : 512 * j_hi],
+            )
+
+        def c_q1(i, t_lo, t_hi):
+            nc.vector.quantize_mx(
+                out=e1c[order[i]][:, 128 * t_lo : 128 * t_hi].bitcast(E5),
+                scales=e1s[order[i]][:, 128 * t_lo : 128 * t_hi],
+                in_=st[("g1", i)][:, 512 * t_lo : 512 * t_hi],
+            )
+
+        def c_small_rj(i):
+            g, a = order[i]
+            if g == 1:
+                nc.vector.tensor_tensor(out=nrj[:, a, :], in0=rjp[:, 0, a, :], in1=rjp[:, 1, a, :], op=ALU.add)
+
+        def c_small_rb(i):
+            g, a = order[i]
+            if a == 3:
+                nc.vector.tensor_reduce(
+                    out=rbs[:, g, :], in_=rbp[:, g].rearrange("p a j -> p j a"), axis=AX.X, op=ALU.add
+                )
+                nc.vector.tensor_scalar_mul(out=nrb[:, g, :], in0=rbs[:, g, :], scalar1=-1.0)
+
+        tasks = []
+        ptr = {"mm": 0, "ep": 0, "ready": 0}
+        parts = {}
+        NACC = 5
+        accs = {}
+        outs = {}
+
+        def issue_mm(k, lo, hi):
+            kind, r, s, h = tasks[k]
+            if lo == 0:
+                acc = acc_ps.tile([P, 512], F32, name="acc", tag="acc")
+                accs[k] = acc
+            acc = accs[k]
+            cols = (512 * h, 512 * h + 512)
+            npass = 4 if kind == 0 else 2
+            for c in range(lo, hi):
+                key = (r, c) if kind == 0 else (c, r)
+                lc = e0c[key] if kind == 0 else e1c[key]
+                ls = e0s[key] if kind == 0 else e1s[key]
+                rc = cc[c] if kind == 0 else xc[c]
+                rs = cs[c] if kind == 0 else xs[c]
+                nc.tensor.matmul_mx(
+                    out=acc[:],
+                    lhsT=lc[:, 128 * s : 128 * s + 128].bitcast(E5),
+                    lhsT_scale=ls[:, 128 * s : 128 * s + 128],
+                    rhs=rc[:, cols[0] : cols[1]].bitcast(E4),
+                    rhs_scale=rs[:, cols[0] : cols[1]],
+                    start=(c == 0),
+                    stop=(c == npass - 1),
+                )
+
+        def do_ep(k):
+            kind, r, s, h = tasks[k]
+            if h == 0:
+                o = stage.tile([P, IN], F32, name="o", tag="o")
+                outs[(kind, r, s)] = o
+            o = outs[(kind, r, s)]
+            raw = x_raw[r] if kind == 0 else c_raw[r]
+            sc = nrb[:, r, s : s + 1] if kind == 0 else nrj[:, r, s : s + 1]
+            nc.vector.scalar_tensor_tensor(
+                out=o[:, 512 * h : 512 * h + 512], in0=raw[:, s, 512 * h : 512 * h + 512], scalar=sc,
+                in1=accs[k][:], op0=ALU.mult, op1=ALU.add,
+            )
+            if h == 1:
+                dst = out0_v[:, r, s, :] if kind == 0 else out1_v[:, r, s, :]
+                nc.sync.dma_start(out=dst, in_=o[:])
+
+        def prefetch():
+            while ptr["mm"] < ptr["ready"] and ptr["mm"] < ptr["ep"] + NACC:
+                k = ptr["mm"]
+                issue_mm(k, parts.get(k, 0), 4 if tasks[k][0] == 0 else 2)
+                ptr["mm"] = k + 1
+
+        def pre_acc():
+            for k in range(ptr["mm"], min(len(tasks), ptr["ep"] + NACC)):
+                if parts.get(k, 0) == 0:
+                    npass = 4 if tasks[k][0] == 0 else 2
+                    issue_mm(k, 0, npass - 1)
+                    parts[k] = npass - 1
+
+        def slot(n_ep):
+            for rep in range(n_ep):
+                prefetch()
+                if ptr["ep"] < ptr["mm"]:
+                    do_ep(ptr["ep"])
+                    ptr["ep"] = ptr["ep"] + 1
+                    prefetch()
+
+        def add_tasks(kind, r, s_lo, s_hi):
+            for s in range(s_lo, s_hi):
+                for h in range(2):
+                    tasks.append((kind, r, s, h))
+
+        prep_plan = [1,2,2,2,1,0,0,0]
+        ep_plan = [[0,0,0,0,0,0,0],[0,0,0,0,0,0,0],[0,0,0,0,1,1,0],[1,2,1,0,1,1,0],[0,0,0,0,1,1,0],[1,2,1,0,1,1,0],[0,0,0,0,1,2,0],[1,2,2,0,0,0,0]]
+        prep_ptr = {"c": 0, "q": 0, "lim": 0}
+
+        def copy_prep(count):
+            for k in range(count):
+                prep_copy(prep_ptr["c"])
+                prep_ptr["c"] = prep_ptr["c"] + 1
+
+        def fill_prep():
+            if prep_ptr["q"] < prep_ptr["lim"]:
+                prep_quant(prep_ptr["q"])
+                prep_ptr["q"] = prep_ptr["q"] + 1
+
+        def after_block(i):
+            gp, ap = order[i]
+            if gp == 1:
+                add_tasks(1, ap, 0, 4)
+            if ap == 3:
+                add_tasks(0, gp, 0, 4)
+            ptr["ready"] = len(tasks)
+            prefetch()
+
+        last = nblk - 1
+        a_max(0)
+        a_hot(0)
+        a_s4(0)
+        a_s2(0)
+        a_n(0)
+        a_n2(0)
+        copy_prep(4)
+        for i in range(last):
+            prep_ptr["lim"] = prep_ptr["c"]
+            ep = ep_plan[i]
+            if i + 3 < nblk:
+                load_pr(i + 3)
+            b_u(i)
+            if i == 0:
+                a_max(i + 1)
+                a_k(0)
+            else:
+                slot(ep[0])
+            b_v(i)
+            if i > 0:
+                a_max(i + 1)
+            slot(ep[1])
+            b_yr(nc.vector, i, 0, 4)
+            a_hot(i + 1)
+            if i > 0:
+                c_q0(i - 1, 0, 4)
+            a_s4(i + 1)
+            slot(ep[2])
+            a_s2(i + 1)
+            if i > 0:
+                c_q1(i - 1, 0, 4)
+                c_small_rb(i - 1)
+                c_small_rj(i - 1)
+                after_block(i - 1)
+            a_n(i + 1)
+            b_e(i, 0)
+            a_n2(i + 1)
+            fill_prep()
+            b_e(i, 1)
+            slot(ep[6])
+            b_e(i, 2)
+            fill_prep()
+            slot(ep[3])
+            b_e(i, 3)
+            b_rjs(i)
+            b_rjt(i)
+            b_g1(i, 0, 4)
+            fill_prep()
+            fill_prep()
+            slot(ep[4])
+            copy_prep(prep_plan[i])
+            slot(ep[5])
+            a_k(i + 1)
+        i = last
+        ep = ep_plan[i]
+        b_u(i)
+        slot(ep[0])
+        b_v(i)
+        slot(ep[1])
+        b_yr(nc.vector, i, 0, 4)
+        slot(ep[2])
+        c_q0(i - 1, 0, 4)
+        add_tasks(0, 1, 0, 4)
+        pre_acc()
+        b_e(i, 0)
+        c_q1(i - 1, 0, 4)
+        b_e(i, 1)
+        c_small_rj(i - 1)
+        add_tasks(1, order[i - 1][1], 0, 4)
+        b_e(i, 2)
+        c_q0(i, 0, 1)
+        b_e(i, 3)
+        b_rjs(i)
+        b_g1(i, 0, 1)
+        b_g1(i, 1, 2)
+        b_rjt(i)
+        b_g1(i, 2, 3)
+        b_g1(i, 3, 4)
+        c_small_rb(i)
+        ptr["ready"] = ptr["ready"] + 2
+        slot(1)
+        c_q0(i, 1, 2)
+        ptr["ready"] = ptr["ready"] + 2
+        slot(2)
+        c_q0(i, 2, 3)
+        ptr["ready"] = ptr["ready"] + 2
+        slot(2)
+        c_q0(i, 3, 4)
+        ptr["ready"] = ptr["ready"] + 10
+        slot(3)
+        c_q1(i, 0, 1)
+        c_q1(i, 1, 2)
+        c_small_rj(i)
+        add_tasks(1, 3, 0, 2)
+        ptr["ready"] = len(tasks)
+        slot(6)
+        c_q1(i, 2, 3)
+        c_q1(i, 3, 4)
+        add_tasks(1, 3, 2, 4)
+        ptr["ready"] = len(tasks)
+        slot(len(tasks))

@@ -29,7 +29,7 @@ def tile_pnn_v_kernel(tc, x, centers, probs, grad_out, out_0, out_1):
     out0_v = out_0.rearrange("(g p j) i -> p g j i", g=2, j=4)
     out1_v = out_1.flatten_outer_dims().rearrange("(a q t) i -> q a t i", a=4, t=4)
 
-    order = [(0, 0), (1, 0), (0, 1), (1, 1), (0, 2), (0, 3), (1, 2), (1, 3)]
+    order = [(0, 0), (1, 0), (0, 1), (0, 2), (0, 3), (1, 1), (1, 2), (1, 3)]
     nblk = len(order)
 
     with ExitStack() as ctx:
@@ -38,13 +38,16 @@ def tile_pnn_v_kernel(tc, x, centers, probs, grad_out, out_0, out_1):
         prp = ctx.enter_context(tc.tile_pool(name="prp", bufs=5))
         work = ctx.enter_context(tc.tile_pool(name="work", bufs=2))
         grp = ctx.enter_context(tc.tile_pool(name="grp", bufs=6))
-        stage = ctx.enter_context(tc.tile_pool(name="stage", bufs=3))
+        stage = ctx.enter_context(tc.tile_pool(name="stage", bufs=6))
         tp_ps = ctx.enter_context(tc.psum_pool(name="tp_ps", bufs=2))
-        acc_ps = ctx.enter_context(tc.psum_pool(name="acc_ps", bufs=5))
+        acc_ps = ctx.enter_context(tc.psum_pool(name="acc_ps", bufs=4))
         rj_ps = ctx.enter_context(tc.psum_pool(name="rj_ps", bufs=1))
+        n_ps = ctx.enter_context(tc.psum_pool(name="n_ps", bufs=1))
 
         ident = const.tile([P, P], F32, name="ident")
         make_identity(nc, ident[:])
+        identb = const.tile([P, P], BF16, name="identb")
+        make_identity(nc, identb[:])
         negones = const.tile([P, P], F32, name="negones")
         nc.gpsimd.memset(negones[:], -1.0)
         dummy = const.tile([P, 1], F32, name="dummy")
@@ -89,6 +92,8 @@ def tile_pnn_v_kernel(tc, x, centers, probs, grad_out, out_0, out_1):
         nrb = keep.tile([P, 2, 4], F32, name="nrb")
         rjp = keep.tile([P, 2, 4, 4], F32, name="rjp")
         nrj = keep.tile([P, 4, 4], F32, name="nrj")
+        rjl = keep.tile([P, 4, 4], F32, name="rjl")
+        rjl2 = keep.tile([P, 4], F32, name="rjl2")
 
         pr_tiles = {}
 
@@ -98,8 +103,11 @@ def tile_pnn_v_kernel(tc, x, centers, probs, grad_out, out_0, out_1):
             nc.sync.dma_start(out=pr[:], in_=probs_v[:, g, :, 512 * a : 512 * a + 512])
             pr_tiles[i] = pr
 
+        pr0 = prp.tile([P, 4, 512], F32, name="pr", tag="pr")
+        pr_tiles[0] = pr0
+        for j in range(4):
+            nc.sync.dma_start(out=pr0[:, j, :], in_=probs_v[:, order[0][0], j, 512 * order[0][1] : 512 * order[0][1] + 512])
         nc.sync.dma_start(out=gt[:], in_=grad_v)
-        load_pr(0)
         load_pr(1)
         nc.sync.dma_start(out=x_raw[0][:], in_=x_v[:, 0])
         nc.sync.dma_start(out=x_raw[1][:], in_=x_v[:, 1])
@@ -133,62 +141,60 @@ def tile_pnn_v_kernel(tc, x, centers, probs, grad_out, out_0, out_1):
         def a_max(i):
             pr = pr_tiles[i]
             m = work.tile([P, 4, 64], F32, name="m", tag="m")
-            nc.vector.tensor_reduce(
-                out=m[:], in_=pr[:].rearrange("p j (o d) -> p j o d", d=8), axis=AX.X, op=ALU.max
-            )
+            pieces = 4 if i == 0 else 1
+            step = 4 // pieces
+            for c in range(pieces):
+                nc.vector.tensor_reduce(
+                    out=m[:, step * c : step * c + step, :],
+                    in_=pr[:, step * c : step * c + step, :].rearrange("p j (o d) -> p j o d", d=8),
+                    axis=AX.X, op=ALU.max,
+                )
             st[("m", i)] = m
 
         def a_hot(i):
             pr = pr_tiles[i]
-            hot = work.tile([P, 4, 8, 64], BF16, name="hot", tag="hot")
+            hot = work.tile([P, 256, 8], BF16, name="hot", tag="hot")
             nc.vector.tensor_tensor(
                 out=hot[:],
-                in0=pr[:].rearrange("p j (o d) -> p j d o", d=8),
-                in1=st[("m", i)][:].unsqueeze(2).to_broadcast([P, 4, 8, 64]),
+                in0=pr[:].rearrange("p j (o d) -> p (j o) d", d=8),
+                in1=st[("m", i)][:].rearrange("p j o -> p (j o)").unsqueeze(2).to_broadcast([P, 256, 8]),
                 op=ALU.is_equal,
             )
             st[("hot", i)] = hot
-            kk = work.tile([P, 4, 8, 64], BF16, name="kk", tag="kk")
+            kk = work.tile([P, 256, 8], BF16, name="kk", tag="kk")
             nc.scalar.mul(out=kk[:], in_=hot[:], mul=9.0)
             st[("kk", i)] = kk
 
         def a_s4(i):
             hot = st[("hot", i)]
-            s4 = work.tile([P, 4, 4, 64], BF16, name="s4", tag="s4")
-            nc.vector.tensor_tensor(out=s4[:], in0=hot[:, :, 0:4, :], in1=hot[:, :, 4:8, :], op=ALU.add)
+            s4 = work.tile([P, 256, 4], BF16, name="s4", tag="s4")
+            nc.vector.tensor_tensor(out=s4[:], in0=hot[:, :, 0:4], in1=hot[:, :, 4:8], op=ALU.add)
             st[("s4", i)] = s4
 
-        def a_s2(i):
+        def a_cnt(i):
             s4 = st[("s4", i)]
-            s2 = work.tile([P, 4, 2, 64], BF16, name="s2", tag="s2")
-            nc.vector.tensor_tensor(out=s2[:], in0=s4[:, :, 0:2, :], in1=s4[:, :, 2:4, :], op=ALU.add)
-            st[("s2", i)] = s2
-
-        def a_n(i):
-            s2 = st[("s2", i)]
-            n = work.tile([P, 4, 64], BF16, name="n", tag="n")
-            nc.vector.tensor_tensor(out=n[:], in0=s2[:, :, 0, :], in1=s2[:, :, 1, :], op=ALU.add)
+            nps = n_ps.tile([P, 256], F32, name="nps", tag="nps")
+            for r in range(4):
+                nc.tensor.matmul(out=nps[:], lhsT=identb[:], rhs=s4[:, :, r], start=(r == 0), stop=(r == 3))
+            n = work.tile([P, 256, 2], BF16, name="n", tag="n")
+            nc.scalar.copy(out=n[:], in_=nps[:].unsqueeze(2).to_broadcast([P, 256, 2]))
             st[("n", i)] = n
-
-        def a_n2(i):
-            n = st[("n", i)]
-            n2 = work.tile([P, 4, 64], BF16, name="n2", tag="n2")
-            nc.vector.tensor_tensor(out=n2[:], in0=n[:], in1=n[:], op=ALU.mult)
-            rt = work.tile([P, 4, 64], F32, name="rt", tag="rt")
+            n2 = work.tile([P, 256], F32, name="n2", tag="n2")
+            nc.scalar.square(out=n2[:], in_=nps[:])
+            rt = work.tile([P, 256], F32, name="rt", tag="rt")
             nc.scalar.activation(out=rt[:], in_=n2[:], func=ACT.Abs_reciprocal_sqrt)
             st[("rt", i)] = rt
 
         def a_k(i):
-            kk = st[("kk", i)]
+            kv = st[("kk", i)][:].rearrange("p c (r w) -> p c r w", w=2)
             nc.vector.tensor_tensor(
-                out=kk[:], in0=kk[:], in1=st[("n", i)][:].unsqueeze(2).to_broadcast([P, 4, 8, 64]),
-                op=ALU.subtract,
+                out=kv, in0=kv, in1=st[("n", i)][:].unsqueeze(2).to_broadcast([P, 256, 4, 2]), op=ALU.subtract
             )
 
         def b_u(i):
-            u = work.tile([P, 4, 64], F32, name="u", tag="u")
+            u = work.tile([P, 256], F32, name="u", tag="u")
             nc.vector.scalar_tensor_tensor(
-                out=u[:], in0=st[("n", i)][:], scalar=1.0, in1=st[("rt", i)][:],
+                out=u[:], in0=st[("n", i)][:, :, 0], scalar=1.0, in1=st[("rt", i)][:],
                 op0=ALU.subtract, op1=ALU.mult,
             )
             st[("u", i)] = u
@@ -197,7 +203,7 @@ def tile_pnn_v_kernel(tc, x, centers, probs, grad_out, out_0, out_1):
             g, a = order[i]
             v = work.tile([P, 4, 64], F32, name="v", tag="v")
             nc.vector.scalar_tensor_tensor(
-                out=v[:], in0=st[("u", i)][:], scalar=1.0, in1=gt[:, g, :, 64 * a : 64 * a + 64],
+                out=v[:], in0=st[("u", i)][:].rearrange("p (j o) -> p j o", j=4), scalar=1.0, in1=gt[:, g, :, 64 * a : 64 * a + 64],
                 op0=ALU.subtract, op1=ALU.mult,
             )
             st[("v", i)] = v
@@ -216,21 +222,25 @@ def tile_pnn_v_kernel(tc, x, centers, probs, grad_out, out_0, out_1):
             if j == 0:
                 g0 = grp.tile([P, 2048], BF16, name="g0", tag="grp", align_bytes=64)
                 st[("g0", i)] = g0
-                rjw = rj_ps.tile([P, 512], F32, name="rjw", tag="rjw")
-                st[("rjw", i)] = rjw
             g0v = st[("g0", i)][:].rearrange("q (j p t) -> q j p t", j=4, t=4)
-            ej = pr[:, j, :].rearrange("p (o d) -> p o d", d=8)
+            ej = pr[:, j, :]
             nc.vector.scalar_tensor_tensor(
-                out=ej, in0=st[("kk", i)][:, j, :, :].rearrange("p d o -> p o d"), scalar=-0.125, in1=ej,
+                out=ej, in0=st[("kk", i)][:, 64 * j : 64 * j + 64, :].rearrange("p o d -> p (o d)"), scalar=-0.125, in1=ej,
                 op0=ALU.mult, op1=ALU.mult, accum_out=rbp[:, g, a, j : j + 1],
-            )
-            nc.tensor.matmul(
-                out=st[("rjw", i)][:], lhsT=negones[:], rhs=pr[:, j, :], start=(j == 0), stop=(j == 3)
             )
             tp = tp_ps.tile([P, 4, P], F32, name="tp", tag="tp")
             for t in range(4):
                 nc.tensor.transpose(tp[:, t, :], pr[:, j, t:512:4], ident[:])
             nc.scalar.copy(out=g0v[:, j], in_=tp[:].rearrange("q t p -> q p t"))
+            st[("tp", j)] = tp
+
+        def b_rjm(i, j):
+            if j == 0:
+                rjw = rj_ps.tile([P, 512], F32, name="rjw", tag="rjw")
+                st[("rjw", i)] = rjw
+            nc.tensor.matmul(
+                out=st[("rjw", i)][:], lhsT=negones[:], rhs=pr_tiles[i][:, j, :], start=(j == 0), stop=(j == 3)
+            )
 
         def b_rjs(i):
             rjs = work.tile([P, 512], F32, name="rjs", tag="rjs")
@@ -268,6 +278,13 @@ def tile_pnn_v_kernel(tc, x, centers, probs, grad_out, out_0, out_1):
                 in_=st[("g1", i)][:, 512 * t_lo : 512 * t_hi],
             )
 
+        def c_rjl(j):
+            nc.vector.tensor_reduce(out=rjl[:, :, j], in_=st[("tp", j)][:], axis=AX.X, op=ALU.add)
+
+        def c_last_rj():
+            nc.vector.tensor_reduce(out=rjl2[:], in_=rjl[:], axis=AX.X, op=ALU.add)
+            nc.vector.tensor_tensor(out=nrj[:, 3, :], in0=rjp[:, 0, 3, :], in1=rjl2[:], op=ALU.subtract)
+
         def c_small_rj(i):
             g, a = order[i]
             if g == 1:
@@ -284,9 +301,8 @@ def tile_pnn_v_kernel(tc, x, centers, probs, grad_out, out_0, out_1):
         tasks = []
         ptr = {"mm": 0, "ep": 0, "ready": 0}
         parts = {}
-        NACC = 5
+        NACC = 4
         accs = {}
-        outs = {}
 
         def issue_mm(k, lo, hi):
             kind, r, s, h = tasks[k]
@@ -314,19 +330,15 @@ def tile_pnn_v_kernel(tc, x, centers, probs, grad_out, out_0, out_1):
 
         def do_ep(k):
             kind, r, s, h = tasks[k]
-            if h == 0:
-                o = stage.tile([P, IN], F32, name="o", tag="o")
-                outs[(kind, r, s)] = o
-            o = outs[(kind, r, s)]
+            cols = (512 * h, 512 * h + 512)
+            o = stage.tile([P, 512], F32, name="o", tag="o")
             raw = x_raw[r] if kind == 0 else c_raw[r]
             sc = nrb[:, r, s : s + 1] if kind == 0 else nrj[:, r, s : s + 1]
             nc.vector.scalar_tensor_tensor(
-                out=o[:, 512 * h : 512 * h + 512], in0=raw[:, s, 512 * h : 512 * h + 512], scalar=sc,
-                in1=accs[k][:], op0=ALU.mult, op1=ALU.add,
+                out=o[:], in0=raw[:, s, cols[0] : cols[1]], scalar=sc, in1=accs[k][:], op0=ALU.mult, op1=ALU.add
             )
-            if h == 1:
-                dst = out0_v[:, r, s, :] if kind == 0 else out1_v[:, r, s, :]
-                nc.sync.dma_start(out=dst, in_=o[:])
+            dst = out0_v[:, r, s, cols[0] : cols[1]] if kind == 0 else out1_v[:, r, s, cols[0] : cols[1]]
+            nc.sync.dma_start(out=dst, in_=o[:])
 
         def prefetch():
             while ptr["mm"] < ptr["ready"] and ptr["mm"] < ptr["ep"] + NACC:
@@ -354,8 +366,8 @@ def tile_pnn_v_kernel(tc, x, centers, probs, grad_out, out_0, out_1):
                 for h in range(2):
                     tasks.append((kind, r, s, h))
 
-        prep_plan = [1,2,2,2,1,0,0,0]
-        ep_plan = [[0,0,0,0,0,0,0],[0,0,0,0,0,0,0],[0,0,0,0,1,1,0],[1,2,1,0,1,1,0],[0,0,0,0,1,1,0],[1,2,1,0,1,1,0],[0,0,0,0,1,2,0],[1,2,2,0,0,0,0]]
+        prep_plan = [2,2,2,2,0,0,0,0]
+        ep_plan = [[0,0,0,0,0],[0,0,0,0,0],[0,0,0,0,0],[1,2,2,0,0],[0,2,1,0,0],[0,0,0,0,2],[1,2,2,0,1],[1,3,4,4,0,0]]
         prep_ptr = {"c": 0, "q": 0, "lim": 0}
 
         def copy_prep(count):
@@ -381,9 +393,7 @@ def tile_pnn_v_kernel(tc, x, centers, probs, grad_out, out_0, out_1):
         a_max(0)
         a_hot(0)
         a_s4(0)
-        a_s2(0)
-        a_n(0)
-        a_n2(0)
+        a_cnt(0)
         copy_prep(4)
         for i in range(last):
             prep_ptr["lim"] = prep_ptr["c"]
@@ -392,90 +402,101 @@ def tile_pnn_v_kernel(tc, x, centers, probs, grad_out, out_0, out_1):
                 load_pr(i + 3)
             b_u(i)
             if i == 0:
-                a_max(i + 1)
                 a_k(0)
             else:
-                slot(ep[0])
+                b_rjm(i - 1, 0)
+            slot(ep[0])
             b_v(i)
             if i > 0:
-                a_max(i + 1)
+                b_rjm(i - 1, 1)
+            a_max(i + 1)
             slot(ep[1])
+            if i > 0:
+                b_rjm(i - 1, 2)
+            slot(ep[2])
+            if i > 0:
+                b_rjm(i - 1, 3)
+                b_rjs(i - 1)
+                b_rjt(i - 1)
             b_yr(nc.vector, i, 0, 4)
             a_hot(i + 1)
             if i > 0:
                 c_q0(i - 1, 0, 4)
+            else:
+                fill_prep()
             a_s4(i + 1)
-            slot(ep[2])
-            a_s2(i + 1)
             if i > 0:
                 c_q1(i - 1, 0, 4)
+            else:
+                fill_prep()
+            a_cnt(i + 1)
+            if i > 0:
                 c_small_rb(i - 1)
-                c_small_rj(i - 1)
                 after_block(i - 1)
-            a_n(i + 1)
+            slot(ep[3])
+            fill_prep()
             b_e(i, 0)
-            a_n2(i + 1)
             fill_prep()
             b_e(i, 1)
-            slot(ep[6])
+            a_k(i + 1)
             b_e(i, 2)
             fill_prep()
-            slot(ep[3])
+            if i > 0:
+                c_small_rj(i - 1)
             b_e(i, 3)
-            b_rjs(i)
-            b_rjt(i)
             b_g1(i, 0, 4)
-            fill_prep()
+            copy_prep(prep_plan[i])
             fill_prep()
             slot(ep[4])
-            copy_prep(prep_plan[i])
-            slot(ep[5])
-            a_k(i + 1)
         i = last
         ep = ep_plan[i]
         b_u(i)
+        b_rjm(i - 1, 0)
+        b_rjm(i - 1, 1)
         slot(ep[0])
         b_v(i)
+        b_rjm(i - 1, 2)
+        b_rjm(i - 1, 3)
+        b_rjs(i - 1)
+        b_rjt(i - 1)
         slot(ep[1])
         b_yr(nc.vector, i, 0, 4)
-        slot(ep[2])
         c_q0(i - 1, 0, 4)
+        c_q1(i - 1, 0, 4)
+        add_tasks(1, order[i - 1][1], 0, 4)
+        ptr["ready"] = len(tasks)
+        prefetch()
+        slot(ep[2])
+        c_small_rj(i - 1)
+        slot(ep[3])
         add_tasks(0, 1, 0, 4)
         pre_acc()
         b_e(i, 0)
-        c_q1(i - 1, 0, 4)
+        slot(ep[4])
+        pre_acc()
         b_e(i, 1)
-        c_small_rj(i - 1)
-        add_tasks(1, order[i - 1][1], 0, 4)
+        slot(ep[5])
+        pre_acc()
+        c_rjl(0)
         b_e(i, 2)
+        c_rjl(1)
         c_q0(i, 0, 1)
         b_e(i, 3)
-        b_rjs(i)
-        b_g1(i, 0, 1)
-        b_g1(i, 1, 2)
-        b_rjt(i)
-        b_g1(i, 2, 3)
-        b_g1(i, 3, 4)
+        b_g1(i, 0, 2)
+        b_g1(i, 2, 4)
         c_small_rb(i)
-        ptr["ready"] = ptr["ready"] + 2
-        slot(1)
+        c_rjl(2)
         c_q0(i, 1, 2)
-        ptr["ready"] = ptr["ready"] + 2
-        slot(2)
-        c_q0(i, 2, 3)
-        ptr["ready"] = ptr["ready"] + 2
-        slot(2)
-        c_q0(i, 3, 4)
-        ptr["ready"] = ptr["ready"] + 10
+        ptr["ready"] = ptr["ready"] + 4
         slot(3)
-        c_q1(i, 0, 1)
-        c_q1(i, 1, 2)
-        c_small_rj(i)
-        add_tasks(1, 3, 0, 2)
-        ptr["ready"] = len(tasks)
-        slot(6)
-        c_q1(i, 2, 3)
-        c_q1(i, 3, 4)
-        add_tasks(1, 3, 2, 4)
+        c_q0(i, 2, 3)
+        c_rjl(3)
+        c_q0(i, 3, 4)
+        ptr["ready"] = ptr["ready"] + 4
+        slot(3)
+        c_last_rj()
+        c_q1(i, 0, 2)
+        c_q1(i, 2, 4)
+        add_tasks(1, 3, 0, 4)
         ptr["ready"] = len(tasks)
         slot(len(tasks))

@@ -367,7 +367,7 @@ def tile_pnn_v_kernel(tc, x, centers, probs, grad_out, out_0, out_1):
                     tasks.append((kind, r, s, h))
 
         prep_plan = [2,2,2,2,0,0,0,0]
-        ep_plan = [[0,0,0,0,0],[0,0,0,0,0],[0,0,0,0,0],[1,2,2,0,0],[0,2,1,0,0],[0,0,0,0,2],[1,2,2,0,1],[1,3,4,4,0,0]]
+        ep_plan = [[0,0,0,0,0],[0,0,0,0,0],[0,0,0,0,0],[0,2,2,0,0],[0,2,2,0,0],[0,0,0,0,2],[0,2,2,0,2],[0,4,4,4,0,0]]
         prep_ptr = {"c": 0, "q": 0, "lim": 0}
 
         def copy_prep(count):
@@ -409,6 +409,9 @@ def tile_pnn_v_kernel(tc, x, centers, probs, grad_out, out_0, out_1):
             b_v(i)
             if i > 0:
                 b_rjm(i - 1, 1)
+            gsplit = [2,2,2,4,4,2,4][i]
+            for j in range(gsplit):
+                b_yr(nc.gpsimd, i, j, j + 1)
             a_max(i + 1)
             slot(ep[1])
             if i > 0:
@@ -418,7 +421,8 @@ def tile_pnn_v_kernel(tc, x, centers, probs, grad_out, out_0, out_1):
                 b_rjm(i - 1, 3)
                 b_rjs(i - 1)
                 b_rjt(i - 1)
-            b_yr(nc.vector, i, 0, 4)
+            if gsplit < 4:
+                b_yr(nc.vector, i, gsplit, 4)
             a_hot(i + 1)
             if i > 0:
                 c_q0(i - 1, 0, 4)
@@ -459,8 +463,10 @@ def tile_pnn_v_kernel(tc, x, centers, probs, grad_out, out_0, out_1):
         b_rjm(i - 1, 3)
         b_rjs(i - 1)
         b_rjt(i - 1)
+        for j in range(4):
+            b_yr(nc.gpsimd, i, j, j + 1)
         slot(ep[1])
-        b_yr(nc.vector, i, 0, 4)
+        slot(0)
         c_q0(i - 1, 0, 4)
         c_q1(i - 1, 0, 4)
         add_tasks(1, order[i - 1][1], 0, 4)

@@ -18,6 +18,7 @@ ACT = mybir.ActivationFunctionType
 AX = mybir.AxisListType
 
 P = 128
+NACC = 4
 
 
 def tile_pnn_v_kernel(tc, x, centers, probs, grad_out, out_0, out_1):
@@ -29,18 +30,18 @@ def tile_pnn_v_kernel(tc, x, centers, probs, grad_out, out_0, out_1):
     out0_v = out_0.rearrange("(g p j) i -> p g j i", g=2, j=4)
     out1_v = out_1.flatten_outer_dims().rearrange("(a q t) i -> q a t i", a=4, t=4)
 
-    order = [(0, 0), (1, 0), (0, 1), (0, 2), (0, 3), (1, 1), (1, 2), (1, 3)]
-    nblk = len(order)
+    slots = [(g, j) for g in range(2) for j in range(4)]
+    nslot = len(slots)
 
     with ExitStack() as ctx:
         const = ctx.enter_context(tc.tile_pool(name="const", bufs=1))
         keep = ctx.enter_context(tc.tile_pool(name="keep", bufs=1))
-        prp = ctx.enter_context(tc.tile_pool(name="prp", bufs=5))
+        cpool = ctx.enter_context(tc.tile_pool(name="cpool", bufs=2))
         work = ctx.enter_context(tc.tile_pool(name="work", bufs=2))
-        grp = ctx.enter_context(tc.tile_pool(name="grp", bufs=6))
-        stage = ctx.enter_context(tc.tile_pool(name="stage", bufs=6))
+        grp = ctx.enter_context(tc.tile_pool(name="grp", bufs=5))
+        stage = ctx.enter_context(tc.tile_pool(name="stage", bufs=7))
         tp_ps = ctx.enter_context(tc.psum_pool(name="tp_ps", bufs=2))
-        acc_ps = ctx.enter_context(tc.psum_pool(name="acc_ps", bufs=4))
+        acc_ps = ctx.enter_context(tc.psum_pool(name="acc_ps", bufs=NACC))
         rj_ps = ctx.enter_context(tc.psum_pool(name="rj_ps", bufs=1))
         n_ps = ctx.enter_context(tc.psum_pool(name="n_ps", bufs=1))
 
@@ -48,28 +49,30 @@ def tile_pnn_v_kernel(tc, x, centers, probs, grad_out, out_0, out_1):
         make_identity(nc, ident[:])
         identb = const.tile([P, P], BF16, name="identb")
         make_identity(nc, identb[:])
-        negones = const.tile([P, P], F32, name="negones")
-        nc.gpsimd.memset(negones[:], -1.0)
+        sel = const.tile([P, 4, P], F32, name="sel")
+        nc.gpsimd.memset(sel[:], 0.0)
+        for a in range(4):
+            nc.gpsimd.memset(sel[:, a, 32 * a : 32 * a + 32], -1.0)
         dummy = const.tile([P, 1], F32, name="dummy")
-        nc.scalar.activation(out=dummy[:], in_=negones[:, 0:1], func=ACT.Abs_reciprocal_sqrt)
+        nc.scalar.activation(out=dummy[:], in_=ident[:, 0:1], func=ACT.Abs_reciprocal_sqrt, bias=1.0)
 
         gt = keep.tile([P, 2, 4, OUT], BF16, name="gt")
+        prg = []
         x_raw = []
         xc = []
         xs = []
         for g in range(2):
+            pg = keep.tile([P, 4, J], F32, name="prg%d" % g)
+            prg.append(pg)
             xr = keep.tile([P, 4, IN], BF16, name="xraw%d" % g)
             x_raw.append(xr)
             xcg = keep.tile([P, IN], U32, name="xc%d" % g, align_bytes=64)
             xc.append(xcg)
             xsg = keep.tile([P, IN], U8, name="xs%d" % g, align_bytes=64)
             xs.append(xsg)
-        c_raw = []
         cc = []
         cs = []
         for a in range(4):
-            cr = keep.tile([P, 4, IN], BF16, name="craw%d" % a)
-            c_raw.append(cr)
             cca = keep.tile([P, IN], U32, name="cc%d" % a, align_bytes=64)
             cc.append(cca)
             csa = keep.tile([P, IN], U8, name="cs%d" % a, align_bytes=64)
@@ -78,86 +81,115 @@ def tile_pnn_v_kernel(tc, x, centers, probs, grad_out, out_0, out_1):
         e0s = {}
         e1c = {}
         e1s = {}
-        for i in range(nblk):
-            t0 = keep.tile([P, 512], U32, name="e0c%d" % i, align_bytes=64)
-            e0c[order[i]] = t0
-            t1 = keep.tile([P, 512], U8, name="e0s%d" % i, align_bytes=64)
-            e0s[order[i]] = t1
-            t2 = keep.tile([P, 512], U32, name="e1c%d" % i, align_bytes=64)
-            e1c[order[i]] = t2
-            t3 = keep.tile([P, 512], U8, name="e1s%d" % i, align_bytes=64)
-            e1s[order[i]] = t3
-        rbp = keep.tile([P, 2, 4, 4], F32, name="rbp")
-        rbs = keep.tile([P, 2, 4], F32, name="rbs")
-        nrb = keep.tile([P, 2, 4], F32, name="nrb")
-        rjp = keep.tile([P, 2, 4, 4], F32, name="rjp")
+        for g in range(2):
+            for r in range(4):
+                t0 = keep.tile([P, 512], U32, name="e0c%d%d" % (g, r), align_bytes=64)
+                e0c[(g, r)] = t0
+                t1 = keep.tile([P, 512], U8, name="e0s%d%d" % (g, r), align_bytes=64)
+                e0s[(g, r)] = t1
+                t2 = keep.tile([P, 512], U32, name="e1c%d%d" % (g, r), align_bytes=64)
+                e1c[(g, r)] = t2
+                t3 = keep.tile([P, 512], U8, name="e1s%d%d" % (g, r), align_bytes=64)
+                e1s[(g, r)] = t3
+        rb = keep.tile([P, 8], F32, name="rb")
+        nrb = keep.tile([P, 8], F32, name="nrb")
         nrj = keep.tile([P, 4, 4], F32, name="nrj")
+        nrj6 = keep.tile([P, 4, 4], F32, name="nrj6")
         rjl = keep.tile([P, 4, 4], F32, name="rjl")
-        rjl2 = keep.tile([P, 4], F32, name="rjl2")
+        rjs = keep.tile([P, 512], F32, name="rjs")
+        rjw = rj_ps.tile([P, 512], F32, name="rjw")
 
-        pr_tiles = {}
+        c_tiles = {}
+
+        def load_c(a):
+            ct = cpool.tile([P, 4, IN], BF16, name="ct", tag="ct")
+            nc.sync.dma_start(out=ct[:], in_=c_v[:, a])
+            c_tiles[a] = ct
 
         def load_pr(i):
-            g, a = order[i]
-            pr = prp.tile([P, 4, 512], F32, name="pr", tag="pr")
-            nc.sync.dma_start(out=pr[:], in_=probs_v[:, g, :, 512 * a : 512 * a + 512])
-            pr_tiles[i] = pr
+            g, j = slots[i]
+            nc.sync.dma_start(out=prg[g][:, j, :], in_=probs_v[:, g, j, :])
 
-        pr0 = prp.tile([P, 4, 512], F32, name="pr", tag="pr")
-        pr_tiles[0] = pr0
-        for j in range(4):
-            nc.sync.dma_start(out=pr0[:, j, :], in_=probs_v[:, order[0][0], j, 512 * order[0][1] : 512 * order[0][1] + 512])
+        for c in range(4):
+            nc.sync.dma_start(out=prg[0][:, 0, 512 * c : 512 * c + 512], in_=probs_v[:, 0, 0, 512 * c : 512 * c + 512])
         nc.sync.dma_start(out=gt[:], in_=grad_v)
         load_pr(1)
-        nc.sync.dma_start(out=x_raw[0][:], in_=x_v[:, 0])
-        nc.sync.dma_start(out=x_raw[1][:], in_=x_v[:, 1])
+        load_c(0)
+        load_c(1)
         load_pr(2)
-        for a in range(4):
-            nc.sync.dma_start(out=c_raw[a][:], in_=c_v[:, a])
+        nc.sync.dma_start(out=x_raw[0][:], in_=x_v[:, 0])
+        load_pr(3)
+        nc.sync.dma_start(out=x_raw[1][:], in_=x_v[:, 1])
+        for i in range(4, nslot):
+            load_pr(i)
 
-        prep = [(x_raw[g], xc[g], xs[g], h) for g in range(2) for h in range(2)]
-        prep.extend([(c_raw[a], cc[a], cs[a], h) for a in range(4) for h in range(2)])
-        prep_tiles = {}
+        jobs = []
+        job_tiles = {}
+        job_ptr = {"c": 0, "q": 0}
 
-        def prep_copy(k):
-            raw, codes, scales, h = prep[k]
-            gq = grp.tile([P, 2048], BF16, name="gq", tag="grp", align_bytes=64)
-            nc.scalar.copy(
-                out=gq[:].rearrange("p (i t) -> p i t", t=4),
-                in_=raw[:, :, 512 * h : 512 * h + 512].rearrange("p t i -> p i t"),
-            )
-            prep_tiles[k] = gq
+        def job_copy(count):
+            for rep in range(count):
+                k = job_ptr["c"]
+                if k < len(jobs):
+                    kind, r, h = jobs[k]
+                    gq = grp.tile([P, 2048], BF16, name="gq", tag="grp", align_bytes=64)
+                    if kind == "e":
+                        nc.scalar.copy(
+                            out=gq[:].rearrange("p (t q j) -> p t q j", t=4, j=4),
+                            in_=prg[r][:, :, 512 * h : 512 * h + 512].rearrange("p j (q t) -> p t q j", t=4),
+                        )
+                    else:
+                        raw = c_tiles[r] if kind == "c" else x_raw[r]
+                        nc.scalar.copy(
+                            out=gq[:].rearrange("p (i t) -> p i t", t=4),
+                            in_=raw[:, :, 512 * h : 512 * h + 512].rearrange("p t i -> p i t"),
+                        )
+                        if kind == "c" and h == 1:
+                            load_c((r + 2) % 4)
+                    job_tiles[k] = gq
+                    job_ptr["c"] = k + 1
 
-        def prep_quant(k):
-            raw, codes, scales, h = prep[k]
-            nc.vector.quantize_mx(
-                out=codes[:, 512 * h : 512 * h + 512].bitcast(E4),
-                scales=scales[:, 512 * h : 512 * h + 512],
-                in_=prep_tiles[k][:],
-            )
+        def job_quant(count):
+            for rep in range(count):
+                k = job_ptr["q"]
+                if k < job_ptr["c"]:
+                    kind, r, h = jobs[k]
+                    if kind == "e":
+                        nc.vector.quantize_mx(out=e1c[(r, h)][:].bitcast(E5), scales=e1s[(r, h)][:], in_=job_tiles[k][:])
+                    else:
+                        codes = cc[r] if kind == "c" else xc[r]
+                        scales = cs[r] if kind == "c" else xs[r]
+                        nc.vector.quantize_mx(
+                            out=codes[:, 512 * h : 512 * h + 512].bitcast(E4),
+                            scales=scales[:, 512 * h : 512 * h + 512],
+                            in_=job_tiles[k][:],
+                        )
+                    job_ptr["q"] = k + 1
 
         st = {}
 
+        def pr_of(i):
+            g, j = slots[i]
+            return prg[g][:, j, :]
+
         def a_max(i):
-            pr = pr_tiles[i]
-            m = work.tile([P, 4, 64], F32, name="m", tag="m")
+            m = work.tile([P, 256], F32, name="m", tag="m")
             pieces = 4 if i == 0 else 1
-            step = 4 // pieces
+            w = 256 // pieces
             for c in range(pieces):
                 nc.vector.tensor_reduce(
-                    out=m[:, step * c : step * c + step, :],
-                    in_=pr[:, step * c : step * c + step, :].rearrange("p j (o d) -> p j o d", d=8),
+                    out=m[:, w * c : w * c + w],
+                    in_=pr_of(i)[:, 8 * w * c : 8 * w * (c + 1)].rearrange("p (o d) -> p o d", d=8),
                     axis=AX.X, op=ALU.max,
                 )
             st[("m", i)] = m
 
         def a_hot(i):
-            pr = pr_tiles[i]
-            hot = work.tile([P, 256, 8], BF16, name="hot", tag="hot")
+            hot = work.tile([P, 256, 8], BF16, name="hot", tag="hot", bufs=1)
             nc.vector.tensor_tensor(
                 out=hot[:],
-                in0=pr[:].rearrange("p j (o d) -> p (j o) d", d=8),
-                in1=st[("m", i)][:].rearrange("p j o -> p (j o)").unsqueeze(2).to_broadcast([P, 256, 8]),
+                in0=pr_of(i).rearrange("p (o d) -> p o d", d=8),
+                in1=st[("m", i)][:].unsqueeze(2).to_broadcast([P, 256, 8]),
                 op=ALU.is_equal,
             )
             st[("hot", i)] = hot
@@ -167,7 +199,7 @@ def tile_pnn_v_kernel(tc, x, centers, probs, grad_out, out_0, out_1):
 
         def a_s4(i):
             hot = st[("hot", i)]
-            s4 = work.tile([P, 256, 4], BF16, name="s4", tag="s4")
+            s4 = work.tile([P, 256, 4], BF16, name="s4", tag="s4", bufs=1)
             nc.vector.tensor_tensor(out=s4[:], in0=hot[:, :, 0:4], in1=hot[:, :, 4:8], op=ALU.add)
             st[("s4", i)] = s4
 
@@ -200,108 +232,61 @@ def tile_pnn_v_kernel(tc, x, centers, probs, grad_out, out_0, out_1):
             st[("u", i)] = u
 
         def b_v(i):
-            g, a = order[i]
-            v = work.tile([P, 4, 64], F32, name="v", tag="v")
+            g, j = slots[i]
+            v = work.tile([P, 256], F32, name="v", tag="v")
             nc.vector.scalar_tensor_tensor(
-                out=v[:], in0=st[("u", i)][:].rearrange("p (j o) -> p j o", j=4), scalar=1.0, in1=gt[:, g, :, 64 * a : 64 * a + 64],
-                op0=ALU.subtract, op1=ALU.mult,
+                out=v[:], in0=st[("u", i)][:], scalar=1.0, in1=gt[:, g, j, :], op0=ALU.subtract, op1=ALU.mult
             )
             st[("v", i)] = v
 
-        def b_yr(eng, i, j_lo, j_hi):
-            prv = pr_tiles[i][:, j_lo:j_hi, :].rearrange("p j (o d) -> p j o d", d=8)
-            eng.tensor_tensor(
-                out=prv, in0=prv,
-                in1=st[("v", i)][:, j_lo:j_hi, :].unsqueeze(3).to_broadcast([P, j_hi - j_lo, 64, 8]),
-                op=ALU.mult,
+        def b_yr(i):
+            prv = pr_of(i).rearrange("p (o d) -> p o d", d=8)
+            nc.vector.tensor_tensor(
+                out=prv, in0=prv, in1=st[("v", i)][:].unsqueeze(2).to_broadcast([P, 256, 8]), op=ALU.mult
             )
 
-        def b_e(i, j):
-            g, a = order[i]
-            pr = pr_tiles[i]
-            if j == 0:
-                g0 = grp.tile([P, 2048], BF16, name="g0", tag="grp", align_bytes=64)
-                st[("g0", i)] = g0
-            g0v = st[("g0", i)][:].rearrange("q (j p t) -> q j p t", j=4, t=4)
-            ej = pr[:, j, :]
+        def b_e(i):
             nc.vector.scalar_tensor_tensor(
-                out=ej, in0=st[("kk", i)][:, 64 * j : 64 * j + 64, :].rearrange("p o d -> p (o d)"), scalar=-0.125, in1=ej,
-                op0=ALU.mult, op1=ALU.mult, accum_out=rbp[:, g, a, j : j + 1],
+                out=pr_of(i), in0=st[("kk", i)][:].rearrange("p o d -> p (o d)"), scalar=-0.125, in1=pr_of(i),
+                op0=ALU.mult, op1=ALU.mult, accum_out=rb[:, i : i + 1],
             )
-            tp = tp_ps.tile([P, 4, P], F32, name="tp", tag="tp")
-            for t in range(4):
-                nc.tensor.transpose(tp[:, t, :], pr[:, j, t:512:4], ident[:])
-            nc.scalar.copy(out=g0v[:, j], in_=tp[:].rearrange("q t p -> q p t"))
-            st[("tp", j)] = tp
+            nc.scalar.mul(out=nrb[:, i : i + 1], in_=rb[:, i : i + 1], mul=-1.0)
 
-        def b_rjm(i, j):
-            if j == 0:
-                rjw = rj_ps.tile([P, 512], F32, name="rjw", tag="rjw")
-                st[("rjw", i)] = rjw
-            nc.tensor.matmul(
-                out=st[("rjw", i)][:], lhsT=negones[:], rhs=pr_tiles[i][:, j, :], start=(j == 0), stop=(j == 3)
-            )
+        def b_tr(i):
+            e = pr_of(i)
+            g0 = grp.tile([P, 2048], BF16, name="g0", tag="grp", align_bytes=64)
+            g0v = g0[:].rearrange("q (a p t) -> q a p t", a=4, t=4)
+            for a in range(4):
+                tp = tp_ps.tile([P, 4, P], F32, name="tp", tag="tp")
+                for t in range(4):
+                    nc.tensor.transpose(tp[:, t, :], e[:, 512 * a + t : 512 * a + 512 : 4], ident[:])
+                nc.scalar.copy(out=g0v[:, a], in_=tp[:].rearrange("q t p -> q p t"))
+                if i == nslot - 1:
+                    nc.vector.tensor_reduce(out=rjl[:, a, :], in_=tp[:], axis=AX.X, op=ALU.add)
+                    nc.vector.tensor_tensor(out=nrj[:, a, :], in0=nrj6[:, a, :], in1=rjl[:, a, :], op=ALU.subtract)
+            st[("g0", i)] = g0
 
-        def b_rjs(i):
-            rjs = work.tile([P, 512], F32, name="rjs", tag="rjs")
-            nc.scalar.copy(out=rjs[:], in_=st[("rjw", i)][:])
-            st[("rjs", i)] = rjs
+        def b_rj(i):
+            e = pr_of(i)
+            for a in range(4):
+                nc.tensor.matmul(
+                    out=rjw[:], lhsT=sel[:, a, :], rhs=e[:, 512 * a : 512 * a + 512],
+                    start=(i == 0 and a == 0), stop=(i == nslot - 2 and a == 3),
+                )
 
-        def b_rjt(i):
-            g, a = order[i]
-            rjs = st[("rjs", i)]
+        def c_q0(i):
+            nc.vector.quantize_mx(out=e0c[slots[i]][:].bitcast(E5), scales=e0s[slots[i]][:], in_=st[("g0", i)][:])
+
+        def d_rj():
+            nc.scalar.copy(out=rjs[:], in_=rjw[:])
             tpr = tp_ps.tile([P, 4, P], F32, name="tpr", tag="tp")
             for t in range(4):
                 nc.tensor.transpose(tpr[:, t, :], rjs[:, t:512:4], ident[:])
-            nc.scalar.copy(out=rjp[:, g, a, :], in_=tpr[:, :, 0])
-
-        def b_g1(i, t_lo, t_hi):
-            if t_lo == 0:
-                g1 = grp.tile([P, 2048], BF16, name="g1", tag="grp", align_bytes=64)
-                st[("g1", i)] = g1
-            nc.scalar.copy(
-                out=st[("g1", i)][:, 512 * t_lo : 512 * t_hi].rearrange("p (t q j) -> p t q j", t=t_hi - t_lo, j=4),
-                in_=pr_tiles[i][:].rearrange("p j (q t) -> p t q j", t=4)[:, t_lo:t_hi],
-            )
-
-        def c_q0(i, j_lo, j_hi):
-            nc.vector.quantize_mx(
-                out=e0c[order[i]][:, 128 * j_lo : 128 * j_hi].bitcast(E5),
-                scales=e0s[order[i]][:, 128 * j_lo : 128 * j_hi],
-                in_=st[("g0", i)][:, 512 * j_lo : 512 * j_hi],
-            )
-
-        def c_q1(i, t_lo, t_hi):
-            nc.vector.quantize_mx(
-                out=e1c[order[i]][:, 128 * t_lo : 128 * t_hi].bitcast(E5),
-                scales=e1s[order[i]][:, 128 * t_lo : 128 * t_hi],
-                in_=st[("g1", i)][:, 512 * t_lo : 512 * t_hi],
-            )
-
-        def c_rjl(j):
-            nc.vector.tensor_reduce(out=rjl[:, :, j], in_=st[("tp", j)][:], axis=AX.X, op=ALU.add)
-
-        def c_last_rj():
-            nc.vector.tensor_reduce(out=rjl2[:], in_=rjl[:], axis=AX.X, op=ALU.add)
-            nc.vector.tensor_tensor(out=nrj[:, 3, :], in0=rjp[:, 0, 3, :], in1=rjl2[:], op=ALU.subtract)
-
-        def c_small_rj(i):
-            g, a = order[i]
-            if g == 1:
-                nc.vector.tensor_tensor(out=nrj[:, a, :], in0=rjp[:, 0, a, :], in1=rjp[:, 1, a, :], op=ALU.add)
-
-        def c_small_rb(i):
-            g, a = order[i]
-            if a == 3:
-                nc.vector.tensor_reduce(
-                    out=rbs[:, g, :], in_=rbp[:, g].rearrange("p a j -> p j a"), axis=AX.X, op=ALU.add
-                )
-                nc.vector.tensor_scalar_mul(out=nrb[:, g, :], in0=rbs[:, g, :], scalar1=-1.0)
+            nc.scalar.copy(out=nrj6[:], in_=tpr[:, :, 0:128:32].rearrange("q t a -> q a t"))
 
         tasks = []
         ptr = {"mm": 0, "ep": 0, "ready": 0}
         parts = {}
-        NACC = 4
         accs = {}
 
         def issue_mm(k, lo, hi):
@@ -313,27 +298,22 @@ def tile_pnn_v_kernel(tc, x, centers, probs, grad_out, out_0, out_1):
             cols = (512 * h, 512 * h + 512)
             npass = 4 if kind == 0 else 2
             for c in range(lo, hi):
-                key = (r, c) if kind == 0 else (c, r)
-                lc = e0c[key] if kind == 0 else e1c[key]
-                ls = e0s[key] if kind == 0 else e1s[key]
+                lc = e0c[(r, s)][:, 128 * c : 128 * c + 128] if kind == 0 else e1c[(c, r)][:, 128 * s : 128 * s + 128]
+                ls = e0s[(r, s)][:, 128 * c : 128 * c + 128] if kind == 0 else e1s[(c, r)][:, 128 * s : 128 * s + 128]
                 rc = cc[c] if kind == 0 else xc[c]
                 rs = cs[c] if kind == 0 else xs[c]
                 nc.tensor.matmul_mx(
-                    out=acc[:],
-                    lhsT=lc[:, 128 * s : 128 * s + 128].bitcast(E5),
-                    lhsT_scale=ls[:, 128 * s : 128 * s + 128],
-                    rhs=rc[:, cols[0] : cols[1]].bitcast(E4),
-                    rhs_scale=rs[:, cols[0] : cols[1]],
-                    start=(c == 0),
-                    stop=(c == npass - 1),
+                    out=acc[:], lhsT=lc.bitcast(E5), lhsT_scale=ls,
+                    rhs=rc[:, cols[0] : cols[1]].bitcast(E4), rhs_scale=rs[:, cols[0] : cols[1]],
+                    start=(c == 0), stop=(c == npass - 1),
                 )
 
         def do_ep(k):
             kind, r, s, h = tasks[k]
             cols = (512 * h, 512 * h + 512)
             o = stage.tile([P, 512], F32, name="o", tag="o")
-            raw = x_raw[r] if kind == 0 else c_raw[r]
-            sc = nrb[:, r, s : s + 1] if kind == 0 else nrj[:, r, s : s + 1]
+            raw = x_raw[r] if kind == 0 else c_tiles[r]
+            sc = nrb[:, 4 * r + s : 4 * r + s + 1] if kind == 0 else nrj[:, r, s : s + 1]
             nc.vector.scalar_tensor_tensor(
                 out=o[:], in0=raw[:, s, cols[0] : cols[1]], scalar=sc, in1=accs[k][:], op0=ALU.mult, op1=ALU.add
             )
@@ -345,13 +325,6 @@ def tile_pnn_v_kernel(tc, x, centers, probs, grad_out, out_0, out_1):
                 k = ptr["mm"]
                 issue_mm(k, parts.get(k, 0), 4 if tasks[k][0] == 0 else 2)
                 ptr["mm"] = k + 1
-
-        def pre_acc():
-            for k in range(ptr["mm"], min(len(tasks), ptr["ep"] + NACC)):
-                if parts.get(k, 0) == 0:
-                    npass = 4 if tasks[k][0] == 0 else 2
-                    issue_mm(k, 0, npass - 1)
-                    parts[k] = npass - 1
 
         def slot(n_ep):
             for rep in range(n_ep):
@@ -365,144 +338,70 @@ def tile_pnn_v_kernel(tc, x, centers, probs, grad_out, out_0, out_1):
             for s in range(s_lo, s_hi):
                 for h in range(2):
                     tasks.append((kind, r, s, h))
-
-        prep_plan = [2,2,2,2,0,0,0,0]
-        ep_plan = [[0,0,0,0,0],[0,0,0,0,0],[0,0,0,0,0],[0,2,2,0,0],[0,2,2,0,0],[0,0,0,0,2],[0,2,2,0,2],[0,4,4,4,0,0]]
-        prep_ptr = {"c": 0, "q": 0, "lim": 0}
-
-        def copy_prep(count):
-            for k in range(count):
-                prep_copy(prep_ptr["c"])
-                prep_ptr["c"] = prep_ptr["c"] + 1
-
-        def fill_prep():
-            if prep_ptr["q"] < prep_ptr["lim"]:
-                prep_quant(prep_ptr["q"])
-                prep_ptr["q"] = prep_ptr["q"] + 1
-
-        def after_block(i):
-            gp, ap = order[i]
-            if gp == 1:
-                add_tasks(1, ap, 0, 4)
-            if ap == 3:
-                add_tasks(0, gp, 0, 4)
             ptr["ready"] = len(tasks)
             prefetch()
 
-        last = nblk - 1
+        jobs.extend([("c", a, h) for a in range(4) for h in range(2)])
+        jobs.extend([("x", 0, h) for h in range(2)])
+        jobs.extend([("e", 0, a) for a in range(4)])
+        jobs.extend([("x", 1, h) for h in range(2)])
+        pending = []
+        EPS = [[0,0,0],[0,0,0],[0,0,0],[0,0,1],[1,2,1],[1,2,1],[1,2,1],[1,2,1]]
         a_max(0)
         a_hot(0)
         a_s4(0)
         a_cnt(0)
-        copy_prep(4)
-        for i in range(last):
-            prep_ptr["lim"] = prep_ptr["c"]
-            ep = ep_plan[i]
-            if i + 3 < nblk:
-                load_pr(i + 3)
+        job_copy(2)
+        a_k(0)
+        for i in range(nslot):
+            nxt = i + 1 < nslot
             b_u(i)
-            if i == 0:
-                a_k(0)
-            else:
-                b_rjm(i - 1, 0)
-            slot(ep[0])
+            slot(EPS[i][0])
             b_v(i)
+            if nxt:
+                a_max(i + 1)
+            slot(EPS[i][1])
+            b_yr(i)
+            if nxt:
+                a_hot(i + 1)
             if i > 0:
-                b_rjm(i - 1, 1)
-            gsplit = [2,2,2,4,4,2,4][i]
-            for j in range(gsplit):
-                b_yr(nc.gpsimd, i, j, j + 1)
-            a_max(i + 1)
-            slot(ep[1])
-            if i > 0:
-                b_rjm(i - 1, 2)
-            slot(ep[2])
-            if i > 0:
-                b_rjm(i - 1, 3)
-                b_rjs(i - 1)
-                b_rjt(i - 1)
-            if gsplit < 4:
-                b_yr(nc.vector, i, gsplit, 4)
-            a_hot(i + 1)
-            if i > 0:
-                c_q0(i - 1, 0, 4)
-            else:
-                fill_prep()
-            a_s4(i + 1)
-            if i > 0:
-                c_q1(i - 1, 0, 4)
-            else:
-                fill_prep()
-            a_cnt(i + 1)
-            if i > 0:
-                c_small_rb(i - 1)
-                after_block(i - 1)
-            slot(ep[3])
-            fill_prep()
-            b_e(i, 0)
-            fill_prep()
-            b_e(i, 1)
-            a_k(i + 1)
-            b_e(i, 2)
-            fill_prep()
-            if i > 0:
-                c_small_rj(i - 1)
-            b_e(i, 3)
-            b_g1(i, 0, 4)
-            copy_prep(prep_plan[i])
-            fill_prep()
-            slot(ep[4])
-        i = last
-        ep = ep_plan[i]
-        b_u(i)
-        b_rjm(i - 1, 0)
-        b_rjm(i - 1, 1)
-        slot(ep[0])
-        b_v(i)
-        b_rjm(i - 1, 2)
-        b_rjm(i - 1, 3)
-        b_rjs(i - 1)
-        b_rjt(i - 1)
-        for j in range(4):
-            b_yr(nc.gpsimd, i, j, j + 1)
-        slot(ep[1])
-        slot(0)
-        c_q0(i - 1, 0, 4)
-        c_q1(i - 1, 0, 4)
-        add_tasks(1, order[i - 1][1], 0, 4)
-        ptr["ready"] = len(tasks)
-        prefetch()
-        slot(ep[2])
-        c_small_rj(i - 1)
-        slot(ep[3])
-        add_tasks(0, 1, 0, 4)
-        pre_acc()
-        b_e(i, 0)
-        slot(ep[4])
-        pre_acc()
-        b_e(i, 1)
-        slot(ep[5])
-        pre_acc()
-        c_rjl(0)
-        b_e(i, 2)
-        c_rjl(1)
-        c_q0(i, 0, 1)
-        b_e(i, 3)
-        b_g1(i, 0, 2)
-        b_g1(i, 2, 4)
-        c_small_rb(i)
-        c_rjl(2)
-        c_q0(i, 1, 2)
-        ptr["ready"] = ptr["ready"] + 4
-        slot(3)
-        c_q0(i, 2, 3)
-        c_rjl(3)
-        c_q0(i, 3, 4)
-        ptr["ready"] = ptr["ready"] + 4
-        slot(3)
-        c_last_rj()
-        c_q1(i, 0, 2)
-        c_q1(i, 2, 4)
-        add_tasks(1, 3, 0, 4)
-        ptr["ready"] = len(tasks)
+                c_q0(i - 1)
+                pending.append(slots[i - 1])
+            if job_ptr["q"] >= 8:
+                for gs in pending:
+                    add_tasks(0, gs[0], gs[1], gs[1] + 1)
+                pending = []
+            if nxt:
+                a_s4(i + 1)
+                a_cnt(i + 1)
+            job_quant(1)
+            b_e(i)
+            if not nxt:
+                job_quant(1)
+            if nxt:
+                b_tr(i)
+                b_rj(i)
+                if i == nslot - 2:
+                    d_rj()
+                job_quant(1)
+                job_copy(2)
+                slot(EPS[i][2])
+                a_k(i + 1)
+        jobs.extend([("e", 1, a) for a in range(4)])
+        job_copy(1)
+        b_tr(nslot - 1)
+        job_copy(1)
+        slot(len(tasks))
+        job_quant(1)
+        add_tasks(1, 0, 0, 4)
+        c_q0(nslot - 1)
+        slot(4)
+        add_tasks(0, 1, 3, 4)
+        for a in range(1, 4):
+            job_copy(1)
+            job_quant(1)
+            slot(len(tasks))
+            if a + 1 < 4:
+                load_c(a + 1)
+            add_tasks(1, a, 0, 4)
         slot(len(tasks))

@@ -19,6 +19,7 @@ AX = mybir.AxisListType
 
 P = 128
 NACC = 4
+FULL_COUNT_SLOTS = 3
 
 
 def tile_pnn_v_kernel(tc, x, centers, probs, grad_out, out_0, out_1):
@@ -199,15 +200,19 @@ def tile_pnn_v_kernel(tc, x, centers, probs, grad_out, out_0, out_1):
 
         def a_s4(i):
             hot = st[("hot", i)]
-            s4 = work.tile([P, 256, 4], BF16, name="s4", tag="s4", bufs=1)
-            nc.vector.tensor_tensor(out=s4[:], in0=hot[:, :, 0:4], in1=hot[:, :, 4:8], op=ALU.add)
-            st[("s4", i)] = s4
+            if i < FULL_COUNT_SLOTS:
+                st[("s4", i)] = hot
+            else:
+                s4 = work.tile([P, 256, 4], BF16, name="s4", tag="s4", bufs=1)
+                nc.vector.tensor_tensor(out=s4[:], in0=hot[:, :, 0:4], in1=hot[:, :, 4:8], op=ALU.add)
+                st[("s4", i)] = s4
 
         def a_cnt(i):
             s4 = st[("s4", i)]
             nps = n_ps.tile([P, 256], F32, name="nps", tag="nps")
-            for r in range(4):
-                nc.tensor.matmul(out=nps[:], lhsT=identb[:], rhs=s4[:, :, r], start=(r == 0), stop=(r == 3))
+            terms = 8 if i < FULL_COUNT_SLOTS else 4
+            for r in range(terms):
+                nc.tensor.matmul(out=nps[:], lhsT=identb[:], rhs=s4[:, :, r], start=(r == 0), stop=(r == terms - 1))
             n = work.tile([P, 256, 2], BF16, name="n", tag="n")
             nc.scalar.copy(out=n[:], in_=nps[:].unsqueeze(2).to_broadcast([P, 256, 2]))
             st[("n", i)] = n

from contextlib import ExitStack

import concourse.mybir as mybir
from concourse.masks import make_identity

B, IN, OUT, ND = 1024, 1024, 256, 8
J = OUT * ND
FLOPS = 2 * 2 * B * J * IN

F32 = mybir.dt.float32
BF16 = mybir.dt.bfloat16
U32 = mybir.dt.uint32
U8 = mybir.dt.uint8
E4 = mybir.dt.float8_e4m3fn_x4
E5 = mybir.dt.float8_e5m2_x4
ALU = mybir.AluOpType
ACT = mybir.ActivationFunctionType
AX = mybir.AxisListType

P = 128
NACC = 4
FULL_COUNT_SLOTS = 3


def tile_pnn_v_kernel(tc, x, centers, probs, grad_out, out_0, out_1):
    nc = tc.nc
    probs_v = probs.rearrange("(g p j) f -> p g j f", g=2, j=4)
    grad_v = grad_out.rearrange("(g p j) o -> p g j o", g=2, j=4)
    x_v = x.rearrange("(g p j) i -> p g j i", g=2, j=4)
    c_v = centers.flatten_outer_dims().rearrange("(a q t) i -> q a t i", a=4, t=4)
    out0_v = out_0.rearrange("(g p j) i -> p g j i", g=2, j=4)
    out1_v = out_1.flatten_outer_dims().rearrange("(a q t) i -> q a t i", a=4, t=4)

    slots = [(g, j) for g in range(2) for j in range(4)]
    nslot = len(slots)

    with ExitStack() as ctx:
        const = ctx.enter_context(tc.tile_pool(name="const", bufs=1))
        keep = ctx.enter_context(tc.tile_pool(name="keep", bufs=1))
        cpool = ctx.enter_context(tc.tile_pool(name="cpool", bufs=2))
        work = ctx.enter_context(tc.tile_pool(name="work", bufs=2))
        grp = ctx.enter_context(tc.tile_pool(name="grp", bufs=5))
        stage = ctx.enter_context(tc.tile_pool(name="stage", bufs=7))
        tp_ps = ctx.enter_context(tc.psum_pool(name="tp_ps", bufs=2))
        acc_ps = ctx.enter_context(tc.psum_pool(name="acc_ps", bufs=NACC))
        rj_ps = ctx.enter_context(tc.psum_pool(name="rj_ps", bufs=1))
        n_ps = ctx.enter_context(tc.psum_pool(name="n_ps", bufs=1))

        ident = const.tile([P, P], F32, name="ident")
        make_identity(nc, ident[:])
        identb = const.tile([P, P], BF16, name="identb")
        make_identity(nc, identb[:])
        sel = const.tile([P, 4, P], F32, name="sel")
        nc.gpsimd.memset(sel[:], 0.0)
        for a in range(4):
            nc.gpsimd.memset(sel[:, a, 32 * a : 32 * a + 32], -1.0)
        dummy = const.tile([P, 1], F32, name="dummy")
        nc.scalar.activation(out=dummy[:], in_=ident[:, 0:1], func=ACT.Abs_reciprocal_sqrt, bias=1.0)

        gt = keep.tile([P, 2, 4, OUT], BF16, name="gt")
        prg = []
        x_raw = []
        xc = []
        xs = []
        for g in range(2):
            pg = keep.tile([P, 4, J], F32, name="prg%d" % g)
            prg.append(pg)
            xr = keep.tile([P, 4, IN], BF16, name="xraw%d" % g)
            x_raw.append(xr)
            xcg = keep.tile([P, IN], U32, name="xc%d" % g, align_bytes=64)
            xc.append(xcg)
            xsg = keep.tile([P, IN], U8, name="xs%d" % g, align_bytes=64)
            xs.append(xsg)
        cc = []
        cs = []
        for a in range(4):
            cca = keep.tile([P, IN], U32, name="cc%d" % a, align_bytes=64)
            cc.append(cca)
            csa = keep.tile([P, IN], U8, name="cs%d" % a, align_bytes=64)
            cs.append(csa)
        e0c = {}
        e0s = {}
        e1c = {}
        e1s = {}
        for g in range(2):
            for r in range(4):
                t0 = keep.tile([P, 512], U32, name="e0c%d%d" % (g, r), align_bytes=64)
                e0c[(g, r)] = t0
                t1 = keep.tile([P, 512], U8, name="e0s%d%d" % (g, r), align_bytes=64)
                e0s[(g, r)] = t1
                t2 = keep.tile([P, 512], U32, name="e1c%d%d" % (g, r), align_bytes=64)
                e1c[(g, r)] = t2
                t3 = keep.tile([P, 512], U8, name="e1s%d%d" % (g, r), align_bytes=64)
                e1s[(g, r)] = t3
        rb = keep.tile([P, 8], F32, name="rb")
        nrb = keep.tile([P, 8], F32, name="nrb")
        nrj = keep.tile([P, 4, 4], F32, name="nrj")
        nrj6 = keep.tile([P, 4, 4], F32, name="nrj6")
        rjl = keep.tile([P, 4, 4], F32, name="rjl")
        rjs = keep.tile([P, 512], F32, name="rjs")
        rjw = rj_ps.tile([P, 512], F32, name="rjw")

        c_tiles = {}

        def load_c(a):
            ct = cpool.tile([P, 4, IN], BF16, name="ct", tag="ct")
            nc.sync.dma_start(out=ct[:], in_=c_v[:, a])
            c_tiles[a] = ct

        def load_pr(i):
            g, j = slots[i]
            nc.sync.dma_start(out=prg[g][:, j, :], in_=probs_v[:, g, j, :])

        for c in range(4):
            nc.sync.dma_start(out=prg[0][:, 0, 512 * c : 512 * c + 512], in_=probs_v[:, 0, 0, 512 * c : 512 * c + 512])
        nc.sync.dma_start(out=gt[:], in_=grad_v)
        load_pr(1)
        load_c(0)
        load_c(1)
        load_pr(2)
        nc.sync.dma_start(out=x_raw[0][:], in_=x_v[:, 0])
        load_pr(3)
        nc.sync.dma_start(out=x_raw[1][:], in_=x_v[:, 1])
        for i in range(4, nslot):
            load_pr(i)

        jobs = []
        job_tiles = {}
        job_ptr = {"c": 0, "q": 0}

        def job_copy(count):
            for rep in range(count):
                k = job_ptr["c"]
                if k < len(jobs):
                    kind, r, h = jobs[k]
                    gq = grp.tile([P, 2048], BF16, name="gq", tag="grp", align_bytes=64)
                    if kind == "e":
                        nc.scalar.copy(
                            out=gq[:].rearrange("p (t q j) -> p t q j", t=4, j=4),
                            in_=prg[r][:, :, 512 * h : 512 * h + 512].rearrange("p j (q t) -> p t q j", t=4),
                        )
                    else:
                        raw = c_tiles[r] if kind == "c" else x_raw[r]
                        nc.scalar.copy(
                            out=gq[:].rearrange("p (i t) -> p i t", t=4),
                            in_=raw[:, :, 512 * h : 512 * h + 512].rearrange("p t i -> p i t"),
                        )
                        if kind == "c" and h == 1:
                            load_c((r + 2) % 4)
                    job_tiles[k] = gq
                    job_ptr["c"] = k + 1

        def job_quant(count):
            for rep in range(count):
                k = job_ptr["q"]
                if k < job_ptr["c"]:
                    kind, r, h = jobs[k]
                    if kind == "e":
                        nc.vector.quantize_mx(out=e1c[(r, h)][:].bitcast(E5), scales=e1s[(r, h)][:], in_=job_tiles[k][:])
                    else:
                        codes = cc[r] if kind == "c" else xc[r]
                        scales = cs[r] if kind == "c" else xs[r]
                        nc.vector.quantize_mx(
                            out=codes[:, 512 * h : 512 * h + 512].bitcast(E4),
                            scales=scales[:, 512 * h : 512 * h + 512],
                            in_=job_tiles[k][:],
                        )
                    job_ptr["q"] = k + 1

        st = {}

        def pr_of(i):
            g, j = slots[i]
            return prg[g][:, j, :]

        def a_max(i):
            m = work.tile([P, 256], F32, name="m", tag="m")
            pieces = 4 if i == 0 else 1
            w = 256 // pieces
            for c in range(pieces):
                nc.vector.tensor_reduce(
                    out=m[:, w * c : w * c + w],
                    in_=pr_of(i)[:, 8 * w * c : 8 * w * (c + 1)].rearrange("p (o d) -> p o d", d=8),
                    axis=AX.X, op=ALU.max,
                )
            st[("m", i)] = m

        def a_hot(i):
            hot = work.tile([P, 256, 8], BF16, name="hot", tag="hot", bufs=1)
            nc.vector.tensor_tensor(
                out=hot[:],
                in0=pr_of(i).rearrange("p (o d) -> p o d", d=8),
                in1=st[("m", i)][:].unsqueeze(2).to_broadcast([P, 256, 8]),
                op=ALU.is_equal,
            )
            st[("hot", i)] = hot
            kk = work.tile([P, 256, 8], BF16, name="kk", tag="kk")
            nc.scalar.mul(out=kk[:], in_=hot[:], mul=9.0)
            st[("kk", i)] = kk

        def a_s4(i):
            hot = st[("hot", i)]
            if i < FULL_COUNT_SLOTS:
                st[("s4", i)] = hot
            else:
                s4 = work.tile([P, 256, 4], BF16, name="s4", tag="s4", bufs=1)
                nc.vector.tensor_tensor(out=s4[:], in0=hot[:, :, 0:4], in1=hot[:, :, 4:8], op=ALU.add)
                st[("s4", i)] = s4

        def a_cnt(i):
            s4 = st[("s4", i)]
            nps = n_ps.tile([P, 256], F32, name="nps", tag="nps")
            terms = 8 if i < FULL_COUNT_SLOTS else 4
            for r in range(terms):
                nc.tensor.matmul(out=nps[:], lhsT=identb[:], rhs=s4[:, :, r], start=(r == 0), stop=(r == terms - 1))
            n = work.tile([P, 256, 2], BF16, name="n", tag="n")
            nc.scalar.copy(out=n[:], in_=nps[:].unsqueeze(2).to_broadcast([P, 256, 2]))
            st[("n", i)] = n
            n2 = work.tile([P, 256], F32, name="n2", tag="n2")
            nc.scalar.square(out=n2[:], in_=nps[:])
            rt = work.tile([P, 256], F32, name="rt", tag="rt")
            nc.scalar.activation(out=rt[:], in_=n2[:], func=ACT.Abs_reciprocal_sqrt)
            st[("rt", i)] = rt

        def a_k(i):
            kv = st[("kk", i)][:].rearrange("p c (r w) -> p c r w", w=2)
            nc.vector.tensor_tensor(
                out=kv, in0=kv, in1=st[("n", i)][:].unsqueeze(2).to_broadcast([P, 256, 4, 2]), op=ALU.subtract
            )

        def b_u(i):
            u = work.tile([P, 256], F32, name="u", tag="u")
            nc.vector.scalar_tensor_tensor(
                out=u[:], in0=st[("n", i)][:, :, 0], scalar=1.0, in1=st[("rt", i)][:],
                op0=ALU.subtract, op1=ALU.mult,
            )
            st[("u", i)] = u

        def b_v(i):
            g, j = slots[i]
            v = work.tile([P, 256], F32, name="v", tag="v")
            nc.vector.scalar_tensor_tensor(
                out=v[:], in0=st[("u", i)][:], scalar=1.0, in1=gt[:, g, j, :], op0=ALU.subtract, op1=ALU.mult
            )
            st[("v", i)] = v

        def b_yr(i):
            prv = pr_of(i).rearrange("p (o d) -> p o d", d=8)
            nc.vector.tensor_tensor(
                out=prv, in0=prv, in1=st[("v", i)][:].unsqueeze(2).to_broadcast([P, 256, 8]), op=ALU.mult
            )

        def b_e(i):
            nc.vector.scalar_tensor_tensor(
                out=pr_of(i), in0=st[("kk", i)][:].rearrange("p o d -> p (o d)"), scalar=-0.125, in1=pr_of(i),
                op0=ALU.mult, op1=ALU.mult, accum_out=rb[:, i : i + 1],
            )
            nc.scalar.mul(out=nrb[:, i : i + 1], in_=rb[:, i : i + 1], mul=-1.0)

        def b_tr(i):
            e = pr_of(i)
            g0 = grp.tile([P, 2048], BF16, name="g0", tag="grp", align_bytes=64)
            g0v = g0[:].rearrange("q (a p t) -> q a p t", a=4, t=4)
            for a in range(4):
                tp = tp_ps.tile([P, 4, P], F32, name="tp", tag="tp")
                for t in range(4):
                    nc.tensor.transpose(tp[:, t, :], e[:, 512 * a + t : 512 * a + 512 : 4], ident[:])
                nc.scalar.copy(out=g0v[:, a], in_=tp[:].rearrange("q t p -> q p t"))
                if i == nslot - 1:
                    nc.vector.tensor_reduce(out=rjl[:, a, :], in_=tp[:], axis=AX.X, op=ALU.add)
                    nc.vector.tensor_tensor(out=nrj[:, a, :], in0=nrj6[:, a, :], in1=rjl[:, a, :], op=ALU.subtract)
            st[("g0", i)] = g0

        def b_rj(i):
            e = pr_of(i)
            for a in range(4):
                nc.tensor.matmul(
                    out=rjw[:], lhsT=sel[:, a, :], rhs=e[:, 512 * a : 512 * a + 512],
                    start=(i == 0 and a == 0), stop=(i == nslot - 2 and a == 3),
                )

        def c_q0(i):
            nc.vector.quantize_mx(out=e0c[slots[i]][:].bitcast(E5), scales=e0s[slots[i]][:], in_=st[("g0", i)][:])

        def d_rj():
            nc.scalar.copy(out=rjs[:], in_=rjw[:])
            tpr = tp_ps.tile([P, 4, P], F32, name="tpr", tag="tp")
            for t in range(4):
                nc.tensor.transpose(tpr[:, t, :], rjs[:, t:512:4], ident[:])
            nc.scalar.copy(out=nrj6[:], in_=tpr[:, :, 0:128:32].rearrange("q t a -> q a t"))

        tasks = []
        ptr = {"mm": 0, "ep": 0, "ready": 0}
        parts = {}
        accs = {}

        def issue_mm(k, lo, hi):
            kind, r, s, h = tasks[k]
            if lo == 0:
                acc = acc_ps.tile([P, 512], F32, name="acc", tag="acc")
                accs[k] = acc
            acc = accs[k]
            cols = (512 * h, 512 * h + 512)
            npass = 4 if kind == 0 else 2
            for c in range(lo, hi):
                lc = e0c[(r, s)][:, 128 * c : 128 * c + 128] if kind == 0 else e1c[(c, r)][:, 128 * s : 128 * s + 128]
                ls = e0s[(r, s)][:, 128 * c : 128 * c + 128] if kind == 0 else e1s[(c, r)][:, 128 * s : 128 * s + 128]
                rc = cc[c] if kind == 0 else xc[c]
                rs = cs[c] if kind == 0 else xs[c]
                nc.tensor.matmul_mx(
                    out=acc[:], lhsT=lc.bitcast(E5), lhsT_scale=ls,
                    rhs=rc[:, cols[0] : cols[1]].bitcast(E4), rhs_scale=rs[:, cols[0] : cols[1]],
                    start=(c == 0), stop=(c == npass - 1),
                )

        def do_ep(k):
            kind, r, s, h = tasks[k]
            cols = (512 * h, 512 * h + 512)
            o = stage.tile([P, 512], F32, name="o", tag="o")
            raw = x_raw[r] if kind == 0 else c_tiles[r]
            sc = nrb[:, 4 * r + s : 4 * r + s + 1] if kind == 0 else nrj[:, r, s : s + 1]
            nc.vector.scalar_tensor_tensor(
                out=o[:], in0=raw[:, s, cols[0] : cols[1]], scalar=sc, in1=accs[k][:], op0=ALU.mult, op1=ALU.add
            )
            dst = out0_v[:, r, s, cols[0] : cols[1]] if kind == 0 else out1_v[:, r, s, cols[0] : cols[1]]
            nc.sync.dma_start(out=dst, in_=o[:])

        def prefetch():
            while ptr["mm"] < ptr["ready"] and ptr["mm"] < ptr["ep"] + NACC:
                k = ptr["mm"]
                issue_mm(k, parts.get(k, 0), 4 if tasks[k][0] == 0 else 2)
                ptr["mm"] = k + 1

        def slot(n_ep):
            for rep in range(n_ep):
                prefetch()
                if ptr["ep"] < ptr["mm"]:
                    do_ep(ptr["ep"])
                    ptr["ep"] = ptr["ep"] + 1
                    prefetch()

        def add_tasks(kind, r, s_lo, s_hi):
            for s in range(s_lo, s_hi):
                for h in range(2):
                    tasks.append((kind, r, s, h))
            ptr["ready"] = len(tasks)
            prefetch()

        jobs.extend([("c", a, h) for a in range(4) for h in range(2)])
        jobs.extend([("x", 0, h) for h in range(2)])
        jobs.extend([("e", 0, a) for a in range(4)])
        jobs.extend([("x", 1, h) for h in range(2)])
        pending = []
        EPS = [[0,0,0],[0,0,0],[0,0,0],[0,0,1],[1,2,1],[1,2,1],[1,2,1],[1,2,1]]
        a_max(0)
        a_hot(0)
        a_s4(0)
        a_cnt(0)
        job_copy(2)
        a_k(0)
        for i in range(nslot):
            nxt = i + 1 < nslot
            b_u(i)
            slot(EPS[i][0])
            b_v(i)
            if nxt:
                a_max(i + 1)
            slot(EPS[i][1])
            b_yr(i)
            if nxt:
                a_hot(i + 1)
            if i > 0:
                c_q0(i - 1)
                pending.append(slots[i - 1])
            if job_ptr["q"] >= 8:
                for gs in pending:
                    add_tasks(0, gs[0], gs[1], gs[1] + 1)
                pending = []
            if nxt:
                a_s4(i + 1)
                a_cnt(i + 1)
            job_quant(1)
            b_e(i)
            if not nxt:
                job_quant(1)
            if nxt:
                b_tr(i)
                b_rj(i)
                if i == nslot - 2:
                    d_rj()
                job_quant(1)
                job_copy(2)
                slot(EPS[i][2])
                a_k(i + 1)
        jobs.extend([("e", 1, a) for a in range(4)])
        job_copy(1)
        b_tr(nslot - 1)
        job_copy(1)
        slot(len(tasks))
        job_quant(1)
        add_tasks(1, 0, 0, 4)
        c_q0(nslot - 1)
        slot(4)
        add_tasks(0, 1, 3, 4)
        for a in range(1, 4):
            job_copy(1)
            job_quant(1)
            slot(len(tasks))
            if a + 1 < 4:
                load_c(a + 1)
            add_tasks(1, a, 0, 4)
        slot(len(tasks))
